import numpy as np
import ml_dtypes


def mxq(x, axis, fmt="e4m3"):
    dtype, down = {"e4m3": (ml_dtypes.float8_e4m3fn, 7), "e5m2": (ml_dtypes.float8_e5m2, 14)}[fmt]
    v = np.moveaxis(np.asarray(x, np.float32).astype(ml_dtypes.bfloat16).astype(np.float64), axis, -1)
    blocks = v.reshape(v.shape[:-1] + (-1, 32))
    amax = np.abs(blocks).max(-1, keepdims=True)
    byte = np.maximum(np.where(amax > 0, np.frexp(amax)[1] - 1 + 127, 0) - down, 1)
    scale = np.exp2(byte - 127.0)
    codes = (blocks / scale).astype(np.float32).astype(dtype).astype(np.float64)
    return np.moveaxis((codes * scale).reshape(v.shape), -1, axis)


WIDE = False


def mx_kscale(k):
    if not WIDE:
        return np.ones(k)
    levels = np.array([10, -10, 5, -5, 0])
    a = np.random.permutation(np.resize(levels, k // 512 * 4)).reshape(k // 512, 4)
    idx = np.arange(k)
    return np.exp2(a[idx // 512, idx % 128 // 32])


BF16 = ml_dtypes.bfloat16


def bf(x):
    return np.asarray(x, np.float32).astype(BF16)


def f64(x):
    return np.asarray(x).astype(np.float64)


B, C, CK, CV, CO, H, W, P1, P2, P3, P4 = 2, 1024, 1024, 128, 1024, 48, 48, 1, 3, 6, 8
PSP_SIZES = (P1, P2, P3, P4)
EPS = 1e-5
N = H * W


def bnrelu(x, gamma, beta, mean, var):
    inv = 1.0 / np.sqrt(var + EPS)
    return np.maximum((x - mean[None, :, None]) * (inv * gamma)[None, :, None] + beta[None, :, None], 0.0)


def psp(x):
    b, c = x.shape[:2]
    outs = []
    for s in PSP_SIZES:
        outs.append(x.reshape(b, c, s, H // s, s, W // s).mean(axis=(3, 5)).reshape(b, c, s * s))
    return np.concatenate(outs, axis=-1)


def setup_inputs():
    s = mx_kscale(C)
    fine = np.random.standard_normal((B, C, H, W))
    coarse = np.random.standard_normal((B, C, P4, P4))
    coarse = np.repeat(np.repeat(coarse, H // P4, axis=2), W // P4, axis=3)
    return {"feats": bf((fine + coarse) * np.sqrt(0.5) * s[None, :, None, None]),
            "Wk": bf(np.random.standard_normal((CK, C)) * 1.5 / np.sqrt(C) / s[None, :]),
            "bk": bf(np.random.standard_normal(CK) * 0.2),
            "gk": bf(1.0 + 0.1 * np.random.standard_normal(CK)),
            "betak": bf(np.random.standard_normal(CK) * 0.2),
            "mk": bf(np.random.standard_normal(CK) * 0.2),
            "vk": bf(np.random.uniform(0.5, 1.5, CK)),
            "Wv": bf(np.random.standard_normal((CV, C)) / np.sqrt(C) / s[None, :]),
            "bv": bf(np.random.standard_normal(CV) * 0.2)}


def reference(feats, Wk, bk, gk, betak, mk, vk, Wv, bv):
    xq = mxq(f64(feats).reshape(B, C, N), 1, "e4m3")
    pre = (mxq(f64(Wk), 1, "e4m3") @ xq) + f64(bk)[None, :, None]
    kf = bnrelu(pre, f64(gk), f64(betak), f64(mk), f64(vk)).reshape(B, CK, H, W)
    keyp = psp(kf)
    val = ((mxq(f64(Wv), 1, "e4m3") @ xq) + f64(bv)[None, :, None]).reshape(B, CV, H, W)
    value = psp(val).transpose(0, 2, 1)
    return kf, keyp, value

@@ -1,0 +1,313 @@
+from contextlib import ExitStack
+
+import concourse.mybir as mybir
+from concourse.masks import make_identity
+
+F32 = mybir.dt.float32
+BF16 = mybir.dt.bfloat16
+U32 = mybir.dt.uint32
+U8 = mybir.dt.uint8
+FP8X4 = mybir.dt.float8_e4m3fn_x4
+ACT = mybir.ActivationFunctionType
+ADD = mybir.AluOpType.add
+AXIS = mybir.AxisListType
+
+P = 128
+PACK = 4
+PASSES = 2
+IMAGES = 2
+SIDE = 48
+HALF_ROWS = 24
+HALF = HALF_ROWS * SIDE
+HALVES = 2 * IMAGES
+KEY_TILES = 8
+VALUE_TILE = 8
+TILES = KEY_TILES + 1
+BANK = 512
+QUANT_MAX = 4096
+BLOCKS = 3
+BLOCK = HALF // BLOCKS
+TOKENS = 110
+AT3, AT6, AT8 = 1, 10, 46
+EPS = 1e-5
+
+FLOPS = 2 * IMAGES * SIDE * SIDE * 1024 * (1024 + 128)
+
+
+def tile_apnb_pa_t_kernel(
+    tc, feats, Wk, bk, gk, betak, mk, vk, Wv, bv, out_0, out_1, out_2
+):
+    nc = tc.nc
+
+    x_view = feats.rearrange("b (g u q e) h w -> b q g u e (h w)", g=PASSES, u=2, e=2)
+    kf_view = out_0.rearrange("b (p m) h w -> b p m (h w)", m=KEY_TILES)
+    keyp_view = out_1.rearrange("b (p m) t -> b p (m t)", m=KEY_TILES)
+
+    with ExitStack() as ctx:
+        consts = ctx.enter_context(tc.tile_pool(name="consts", bufs=1))
+        xraw_pool = ctx.enter_context(tc.tile_pool(name="xraw", bufs=3))
+        grouped_pool = ctx.enter_context(tc.tile_pool(name="grouped", bufs=3))
+        xq_pool = ctx.enter_context(tc.tile_pool(name="xq", bufs=2))
+        wstage = ctx.enter_context(tc.tile_pool(name="wstage", bufs=2))
+        kf_pool = ctx.enter_context(tc.tile_pool(name="kf", bufs=3))
+        pool_tmp = ctx.enter_context(tc.tile_pool(name="pool_tmp", bufs=2))
+        sums_pool = ctx.enter_context(tc.tile_pool(name="sums", bufs=2))
+        psum = ctx.enter_context(tc.psum_pool(name="psum", bufs=7))
+
+        ident = consts.tile([P, P], F32)
+        make_identity(nc, ident[:])
+
+        prm = consts.tile([P, 6, 16], BF16)
+        with nc.allow_non_contiguous_dma(reason="8 channels (16 bytes) to a partition"):
+            for slot, vec in enumerate((bk, gk, betak, mk, vk)):
+                nc.scalar.dma_start(
+                    out=prm[:, slot, 0:KEY_TILES],
+                    in_=vec.rearrange("(p m) -> p m", m=KEY_TILES),
+                )
+            nc.scalar.dma_start(out=prm[:, 5, 0:1], in_=bv.rearrange("(p o) -> p o", o=1))
+
+        xraw = {}
+
+        def load_x(half, piece):
+            if piece == 0:
+                xraw[half] = xraw_pool.tile([P, PASSES, PACK, HALF], BF16, name="xraw")
+            g, u = divmod(piece, 2)
+            first = (half % 2) * HALF
+            nc.sync.dma_start(
+                out=xraw[half][:, g, 2 * u : 2 * u + 2, :],
+                in_=x_view[half // 2, :, g, u, :, first : first + HALF],
+            )
+
+        for piece in range(4):
+            load_x(0, piece)
+        wv_raw = consts.tile([P, 1024], BF16)
+        nc.sync.dma_start(out=wv_raw[:], in_=Wv)
+        wk_raw = consts.tile([P, KEY_TILES, 1024], BF16)
+        wk_view = Wk.rearrange("(p m) k -> p m k", m=KEY_TILES)
+        for m in range(0, KEY_TILES, 2):
+            nc.sync.dma_start(out=wk_raw[:, m : m + 2, :], in_=wk_view[:, m : m + 2, :])
+        for piece in range(4):
+            load_x(1, piece)
+
+        scale_t = consts.tile([P, TILES], F32)
+        bias_t = consts.tile([P, TILES], F32)
+        std = consts.tile([P, KEY_TILES], F32)
+        keys = slice(0, KEY_TILES)
+        nc.vector.tensor_scalar_add(out=std[:], in0=prm[:, 4, keys], scalar1=EPS)
+        nc.scalar.sqrt(out=std[:], in_=std[:])
+        nc.vector.reciprocal(out=std[:], in_=std[:])
+        nc.vector.tensor_mul(out=scale_t[:, keys], in0=std[:], in1=prm[:, 1, keys])
+        nc.vector.tensor_sub(out=bias_t[:, keys], in0=prm[:, 0, keys], in1=prm[:, 3, keys])
+        nc.vector.tensor_mul(out=bias_t[:, keys], in0=bias_t[:, keys], in1=scale_t[:, keys])
+        nc.vector.tensor_add(out=bias_t[:, keys], in0=bias_t[:, keys], in1=prm[:, 2, keys])
+        nc.vector.memset(scale_t[:, VALUE_TILE : VALUE_TILE + 1], 1.0)
+        nc.vector.tensor_copy(out=bias_t[:, VALUE_TILE : VALUE_TILE + 1], in_=prm[:, 5, 0:1])
+
+        grouped = {}
+        x_codes = {}
+        x_scales = {}
+
+        def regroup_x(half, g, block, copy):
+            if block == 0:
+                grouped[half, g] = grouped_pool.tile(
+                    [P, HALF, PACK], BF16, name="grouped", align_bytes=64
+                )
+            cols = slice(block * BLOCK, (block + 1) * BLOCK)
+            copy(
+                out=grouped[half, g][:, cols, :].rearrange("p (c i) t -> p c t i", i=4),
+                in_=xraw[half][:, g, :, cols].rearrange("p t (c i) -> p c t i", i=4),
+            )
+
+        def quantise_x(half, g):
+            if g == 0:
+                x_codes[half] = xq_pool.tile([P, PASSES, HALF], U32, name="x_codes", align_bytes=64)
+                x_scales[half] = xq_pool.tile([P, PASSES, HALF], U8, name="x_scales", align_bytes=64)
+            flat = grouped[half, g][:].rearrange("p n t -> p (n t)")
+            for first in range(0, HALF * PACK, QUANT_MAX):
+                width = min(QUANT_MAX, HALF * PACK - first)
+                words = slice(first // PACK, (first + width) // PACK)
+                nc.vector.quantize_mx(
+                    out=x_codes[half][:, g, words].bitcast(FP8X4),
+                    scales=x_scales[half][:, g, words],
+                    in_=flat[:, first : first + width],
+                )
+
+        w_codes = consts.tile([P, TILES, PASSES * P], U32, align_bytes=64)
+        w_scales = consts.tile([P, TILES, PASSES * P], U8, align_bytes=64)
+
+        def prepare_weights(m):
+            rows = wv_raw[:] if m == VALUE_TILE else wk_raw[:, m, :]
+            words = rows.bitcast(F32)
+            turned = psum.tile([P, BANK], F32, tag="acc")
+            for gu in range(PASSES * 2):
+                nc.tensor.transpose(
+                    turned[:, gu * P : (gu + 1) * P], words[:, gu * P : (gu + 1) * P], ident[:]
+                )
+            w_grouped = wstage.tile([P, PASSES, P, PACK], BF16, align_bytes=64)
+            nc.scalar.copy(
+                out=w_grouped[:].bitcast(F32),
+                in_=turned[:].rearrange("q (g u c) -> q g c u", g=PASSES, u=2),
+            )
+            nc.vector.quantize_mx(
+                out=w_codes[:, m, :].bitcast(FP8X4),
+                scales=w_scales[:, m, :],
+                in_=w_grouped[:].rearrange("q g c t -> q (g c t)"),
+            )
+
+        def project(half, tiles):
+            kf = kf_pool.tile([P, len(tiles), HALF], F32, name="kf")
+            for j, m in enumerate(tiles):
+                for first in range(0, HALF, BANK):
+                    width = min(BANK, HALF - first)
+                    acc = psum.tile([P, BANK], F32, tag="acc")
+                    for g in range(PASSES):
+                        nc.tensor.matmul_mx(
+                            out=acc[:, 0:width],
+                            lhsT=w_codes[:, m, g * P : (g + 1) * P].bitcast(FP8X4),
+                            lhsT_scale=w_scales[:, m, g * P : (g + 1) * P],
+                            rhs=x_codes[half][:, g, first : first + width].bitcast(FP8X4),
+                            rhs_scale=x_scales[half][:, g, first : first + width],
+                            start=(g == 0),
+                            stop=(g == PASSES - 1),
+                        )
+                    nc.scalar.activation(
+                        out=kf[:, j, first : first + width],
+                        in_=acc[:, 0:width],
+                        func=ACT.Identity if m == VALUE_TILE else ACT.Relu,
+                        bias=bias_t[:, m : m + 1],
+                        scale=scale_t[:, m : m + 1],
+                    )
+            if tiles[0] != VALUE_TILE:
+                first = (half % 2) * HALF
+                nc.sync.dma_start(
+                    out=kf_view[half // 2, :, tiles[0] : tiles[0] + len(tiles), first : first + HALF],
+                    in_=kf[:],
+                )
+            return kf
+
+        sums8 = {}
+        sums6 = {}
+
+        def add_row_pairs(work):
+            kf = work["kf"]
+            pairs = pool_tmp.tile([P, len(work["tiles"]) * HALF_ROWS // 2, SIDE], F32, name="row_pairs")
+            rows = kf[:].rearrange("p n (a two w) -> p (n a) two w", two=2, w=SIDE)
+            nc.vector.tensor_tensor(out=pairs[:], in0=rows[:, :, 0, :], in1=rows[:, :, 1, :], op=ADD)
+            work["row_pairs"] = pairs
+
+        def add_column_pairs(work):
+            pairs = work["row_pairs"]
+            quads = pool_tmp.tile([P, len(work["tiles"]) * HALF // 4], F32, name="quads")
+            cols = pairs[:].rearrange("p a (c two) -> p (a c) two", two=2)
+            nc.vector.tensor_tensor(out=quads[:], in0=cols[:, :, 0], in1=cols[:, :, 1], op=ADD)
+            work["quads"] = quads
+
+        def sum_cells(work):
+            half, tiles, quads = work["half"], work["tiles"], work["quads"]
+            b, part = divmod(half, 2)
+            if part == 0 and tiles[0] == VALUE_TILE:
+                sums8[b] = sums_pool.tile([P, 2, TILES, 32], F32, name="sums8")
+                sums6[b] = sums_pool.tile([P, 2, TILES, 18], F32, name="sums6")
+            span = slice(tiles[0], tiles[0] + len(tiles))
+            nc.vector.tensor_reduce(
+                out=sums8[b][:, part, span, :].rearrange("p n (r c) -> p (n r) c", c=8),
+                in_=quads[:].rearrange("p (r hi c wi) -> p r c hi wi", hi=3, c=8, wi=3),
+                axis=AXIS.XY,
+                op=ADD,
+            )
+            nc.vector.tensor_reduce(
+                out=sums6[b][:, part, span, :].rearrange("p n (r c) -> p (n r) c", c=6),
+                in_=quads[:].rearrange("p (r hi c wi) -> p r c hi wi", hi=4, c=6, wi=4),
+                axis=AXIS.XY,
+                op=ADD,
+            )
+
+        def finish_image(b):
+            tok = sums_pool.tile([P, KEY_TILES * TOKENS + P], F32, name="tok")
+            nc.vector.memset(tok[:, TILES * TOKENS :], 0.0)
+            by_tile = tok[:, 0 : TILES * TOKENS].rearrange("p (m t) -> p m t", t=TOKENS)
+            level8 = by_tile[:, :, AT8:TOKENS]
+            level6 = by_tile[:, :, AT6:AT8]
+            nc.vector.tensor_scalar_mul(
+                out=level8.rearrange("p m (h j) -> p h m j", h=2), in0=sums8[b][:], scalar1=1.0 / 36.0
+            )
+            nc.vector.tensor_scalar_mul(
+                out=level6.rearrange("p m (h j) -> p h m j", h=2), in0=sums6[b][:], scalar1=1.0 / 64.0
+            )
+            wide = sums_pool.tile([P, TILES, 18], F32, name="wide")
+            nc.vector.tensor_reduce(
+                out=wide[:], in_=level6.rearrange("p m (a wi) -> p m a wi", wi=2), axis=AXIS.X, op=ADD
+            )
+            cells3 = sums_pool.tile([P, TILES * 3, 3], F32, name="cells3")
+            nc.vector.tensor_reduce(
+                out=cells3[:],
+                in_=wide[:].rearrange("p m (r hi c) -> p (m r) c hi", hi=2, c=3),
+                axis=AXIS.X,
+                op=ADD,
+            )
+            nine = cells3[:].rearrange("p (m r) c -> p m (r c)", m=TILES)
+            nc.vector.tensor_scalar_mul(out=by_tile[:, :, AT3:AT6], in0=nine, scalar1=0.25)
+            whole = sums_pool.tile([P, TILES], F32, name="whole")
+            nc.vector.tensor_reduce(out=whole[:], in_=nine, axis=AXIS.X, op=ADD)
+            nc.vector.tensor_scalar_mul(
+                out=by_tile[:, :, 0:AT3], in0=whole[:].unsqueeze(2), scalar1=1.0 / 36.0
+            )
+            nc.sync.dma_start(out=keyp_view[b], in_=tok[:, 0 : KEY_TILES * TOKENS])
+            return tok
+
+        def store_value(b, tok):
+            turned = psum.tile([P, P], F32, tag="value", bufs=1)
+            nc.tensor.transpose(turned[:], tok[:, KEY_TILES * TOKENS :], ident[:])
+            value = sums_pool.tile([P, P], F32, name="value")
+            nc.vector.tensor_copy(out=value[:], in_=turned[:])
+            nc.sync.dma_start(out=out_2[b], in_=value[0:TOKENS, :])
+
+        groups = [[VALUE_TILE]] + [[m, m + 1] for m in range(0, KEY_TILES, 2)]
+        tile_order = [m for tiles in groups for m in tiles]
+
+        for g in range(PASSES):
+            regroup_x(0, g, 0, nc.vector.tensor_copy)
+            regroup_x(0, g, 1, nc.vector.tensor_copy)
+            regroup_x(0, g, 2, nc.scalar.copy)
+            if g > 0:
+                quantise_x(0, g - 1)
+        prepare_weights(tile_order[0])
+        quantise_x(0, PASSES - 1)
+
+        previous = None
+        value_due = None
+        for half in range(HALVES):
+            following = half + 1
+            for step, tiles in enumerate(groups):
+                if half == 0 and step + 1 < len(groups):
+                    for m in groups[step + 1]:
+                        prepare_weights(m)
+                if half + 2 < HALVES and step < 4:
+                    load_x(half + 2, step)
+                if following < HALVES and step >= 2 and step % 2 == 0:
+                    quantise_x(following, step // 2 - 1)
+
+                work = {"half": half, "tiles": tiles, "kf": project(half, tiles)}
+                if value_due is not None:
+                    store_value(value_due[0], value_due[1])
+                    value_due = None
+
+                if previous is not None:
+                    add_column_pairs(previous)
+                add_row_pairs(work)
+                if previous is not None:
+                    sum_cells(previous)
+                    if previous["half"] % 2 == 1 and previous["tiles"] == groups[-1]:
+                        b = previous["half"] // 2
+                        value_due = (b, finish_image(b))
+                previous = work
+
+                if following < HALVES and step < 2 * PASSES:
+                    g = step // 2
+                    regroup_x(following, g, step % 2, nc.scalar.copy)
+                    if step % 2 == 1:
+                        regroup_x(following, g, 2, nc.vector.tensor_copy)
+
+        add_column_pairs(previous)
+        sum_cells(previous)
+        store_value(IMAGES - 1, finish_image(IMAGES - 1))

@@ -68,20 +68,23 @@ def tile_apnb_pa_t_kernel(
 
         xraw = {}
 
-        def load_x(half, piece):
-            if piece == 0:
+        def load_x(half, piece, start=0, width=HALF):
+            if half not in xraw:
                 xraw[half] = xraw_pool.tile([P, PASSES, PACK, HALF], BF16, name="xraw")
             g, u = divmod(piece, 2)
             first = (half % 2) * HALF
             nc.sync.dma_start(
-                out=xraw[half][:, g, 2 * u : 2 * u + 2, :],
-                in_=x_view[half // 2, :, g, u, :, first : first + HALF],
+                out=xraw[half][:, g, 2 * u : 2 * u + 2, start : start + width],
+                in_=x_view[half // 2, :, g, u, :, first + start : first + start + width],
             )
 
-        for piece in range(4):
-            load_x(0, piece)
         wv_raw = consts.tile([P, 1024], BF16)
-        nc.sync.dma_start(out=wv_raw[:], in_=Wv)
+        for g in range(PASSES):
+            for block in range(BLOCKS):
+                for u in range(2):
+                    load_x(0, 2 * g + u, block * BLOCK, BLOCK)
+            if g == 0:
+                nc.sync.dma_start(out=wv_raw[:], in_=Wv)
         wk_raw = consts.tile([P, KEY_TILES, 1024], BF16)
         wk_view = Wk.rearrange("(p m) k -> p m k", m=KEY_TILES)
         for m in range(0, KEY_TILES, 2):
@@ -224,15 +227,15 @@ def tile_apnb_pa_t_kernel(
 
         def finish_image(b):
             tok = sums_pool.tile([P, KEY_TILES * TOKENS + P], F32, name="tok")
-            nc.vector.memset(tok[:, TILES * TOKENS :], 0.0)
+            nc.vector.memset(tok[:, KEY_TILES * TOKENS :], 0.0)
             by_tile = tok[:, 0 : TILES * TOKENS].rearrange("p (m t) -> p m t", t=TOKENS)
             level8 = by_tile[:, :, AT8:TOKENS]
             level6 = by_tile[:, :, AT6:AT8]
-            nc.vector.tensor_scalar_mul(
-                out=level8.rearrange("p m (h j) -> p h m j", h=2), in0=sums8[b][:], scalar1=1.0 / 36.0
+            nc.scalar.mul(
+                out=level6.rearrange("p m (h j) -> p h m j", h=2), in_=sums6[b][:], mul=1.0 / 64.0
             )
-            nc.vector.tensor_scalar_mul(
-                out=level6.rearrange("p m (h j) -> p h m j", h=2), in0=sums6[b][:], scalar1=1.0 / 64.0
+            nc.scalar.mul(
+                out=level8.rearrange("p m (h j) -> p h m j", h=2), in_=sums8[b][:], mul=1.0 / 36.0
             )
             wide = sums_pool.tile([P, TILES, 18], F32, name="wide")
             nc.vector.tensor_reduce(
@@ -246,12 +249,10 @@ def tile_apnb_pa_t_kernel(
                 op=ADD,
             )
             nine = cells3[:].rearrange("p (m r) c -> p m (r c)", m=TILES)
-            nc.vector.tensor_scalar_mul(out=by_tile[:, :, AT3:AT6], in0=nine, scalar1=0.25)
+            nc.scalar.mul(out=by_tile[:, :, AT3:AT6], in_=nine, mul=0.25)
             whole = sums_pool.tile([P, TILES], F32, name="whole")
             nc.vector.tensor_reduce(out=whole[:], in_=nine, axis=AXIS.X, op=ADD)
-            nc.vector.tensor_scalar_mul(
-                out=by_tile[:, :, 0:AT3], in0=whole[:].unsqueeze(2), scalar1=1.0 / 36.0
-            )
+            nc.scalar.mul(out=by_tile[:, :, 0:AT3], in_=whole[:].unsqueeze(2), mul=1.0 / 36.0)
             nc.sync.dma_start(out=keyp_view[b], in_=tok[:, 0 : KEY_TILES * TOKENS])
             return tok
 
@@ -259,7 +260,7 @@ def tile_apnb_pa_t_kernel(
             turned = psum.tile([P, P], F32, tag="value", bufs=1)
             nc.tensor.transpose(turned[:], tok[:, KEY_TILES * TOKENS :], ident[:])
             value = sums_pool.tile([P, P], F32, name="value")
-            nc.vector.tensor_copy(out=value[:], in_=turned[:])
+            nc.scalar.copy(out=value[:], in_=turned[:])
             nc.sync.dma_start(out=out_2[b], in_=value[0:TOKENS, :])
 
         groups = [[VALUE_TILE]] + [[m, m + 1] for m in range(0, KEY_TILES, 2)]

@@ -50,7 +50,7 @@ def tile_apnb_pa_t_kernel(
         xq_pool = ctx.enter_context(tc.tile_pool(name="xq", bufs=2))
         wstage = ctx.enter_context(tc.tile_pool(name="wstage", bufs=2))
         kf_pool = ctx.enter_context(tc.tile_pool(name="kf", bufs=3))
-        pool_tmp = ctx.enter_context(tc.tile_pool(name="pool_tmp", bufs=2))
+        pool_tmp = ctx.enter_context(tc.tile_pool(name="pool_tmp", bufs=3))
         sums_pool = ctx.enter_context(tc.tile_pool(name="sums", bufs=2))
         psum = ctx.enter_context(tc.psum_pool(name="psum", bufs=7))
 
@@ -202,7 +202,7 @@ def tile_apnb_pa_t_kernel(
             pairs = work["row_pairs"]
             quads = pool_tmp.tile([P, len(work["tiles"]) * HALF // 4], F32, name="quads")
             cols = pairs[:].rearrange("p a (c two) -> p (a c) two", two=2)
-            nc.vector.tensor_tensor(out=quads[:], in0=cols[:, :, 0], in1=cols[:, :, 1], op=ADD)
+            nc.gpsimd.tensor_tensor(out=quads[:], in0=cols[:, :, 0], in1=cols[:, :, 1], op=ADD)
             work["quads"] = quads
 
         def sum_cells(work):
@@ -276,6 +276,7 @@ def tile_apnb_pa_t_kernel(
         quantise_x(0, PASSES - 1)
 
         previous = None
+        before = None
         value_due = None
         for half in range(HALVES):
             following = half + 1
@@ -296,19 +297,21 @@ def tile_apnb_pa_t_kernel(
                 if previous is not None:
                     add_column_pairs(previous)
                 add_row_pairs(work)
-                if previous is not None:
-                    sum_cells(previous)
-                    if previous["half"] % 2 == 1 and previous["tiles"] == groups[-1]:
-                        b = previous["half"] // 2
+                if before is not None:
+                    sum_cells(before)
+                    if before["half"] % 2 == 1 and before["tiles"] == groups[-1]:
+                        b = before["half"] // 2
                         value_due = (b, finish_image(b))
+                before = previous
                 previous = work
 
                 if following < HALVES and step < 2 * PASSES:
                     g = step // 2
-                    regroup_x(following, g, step % 2, nc.scalar.copy)
+                    regroup_x(following, g, step % 2, nc.scalar.copy if step % 2 == 0 else nc.vector.tensor_copy)
                     if step % 2 == 1:
                         regroup_x(following, g, 2, nc.vector.tensor_copy)
 
         add_column_pairs(previous)
+        sum_cells(before)
         sum_cells(previous)
         store_value(IMAGES - 1, finish_image(IMAGES - 1))

from contextlib import ExitStack

import concourse.mybir as mybir
from concourse.masks import make_identity

F32 = mybir.dt.float32
BF16 = mybir.dt.bfloat16
U32 = mybir.dt.uint32
U8 = mybir.dt.uint8
FP8X4 = mybir.dt.float8_e4m3fn_x4
ACT = mybir.ActivationFunctionType
ADD = mybir.AluOpType.add
AXIS = mybir.AxisListType

P = 128
PACK = 4
PASSES = 2
IMAGES = 2
SIDE = 48
HALF_ROWS = 24
HALF = HALF_ROWS * SIDE
HALVES = 2 * IMAGES
KEY_TILES = 8
VALUE_TILE = 8
TILES = KEY_TILES + 1
BANK = 512
QUANT_MAX = 4096
BLOCKS = 3
BLOCK = HALF // BLOCKS
TOKENS = 110
AT3, AT6, AT8 = 1, 10, 46
EPS = 1e-5

FLOPS = 2 * IMAGES * SIDE * SIDE * 1024 * (1024 + 128)


def tile_apnb_pa_t_kernel(
    tc, feats, Wk, bk, gk, betak, mk, vk, Wv, bv, out_0, out_1, out_2
):
    nc = tc.nc

    x_view = feats.rearrange("b (g u q e) h w -> b q g u e (h w)", g=PASSES, u=2, e=2)
    kf_view = out_0.rearrange("b (p m) h w -> b p m (h w)", m=KEY_TILES)
    keyp_view = out_1.rearrange("b (p m) t -> b p (m t)", m=KEY_TILES)

    with ExitStack() as ctx:
        consts = ctx.enter_context(tc.tile_pool(name="consts", bufs=1))
        xraw_pool = ctx.enter_context(tc.tile_pool(name="xraw", bufs=3))
        grouped_pool = ctx.enter_context(tc.tile_pool(name="grouped", bufs=3))
        xq_pool = ctx.enter_context(tc.tile_pool(name="xq", bufs=2))
        wstage = ctx.enter_context(tc.tile_pool(name="wstage", bufs=2))
        kf_pool = ctx.enter_context(tc.tile_pool(name="kf", bufs=3))
        pool_tmp = ctx.enter_context(tc.tile_pool(name="pool_tmp", bufs=3))
        sums_pool = ctx.enter_context(tc.tile_pool(name="sums", bufs=2))
        psum = ctx.enter_context(tc.psum_pool(name="psum", bufs=7))

        ident = consts.tile([P, P], F32)
        make_identity(nc, ident[:])

        prm = consts.tile([P, 6, 16], BF16)
        with nc.allow_non_contiguous_dma(reason="8 channels (16 bytes) to a partition"):
            for slot, vec in enumerate((bk, gk, betak, mk, vk)):
                nc.scalar.dma_start(
                    out=prm[:, slot, 0:KEY_TILES],
                    in_=vec.rearrange("(p m) -> p m", m=KEY_TILES),
                )
            nc.scalar.dma_start(out=prm[:, 5, 0:1], in_=bv.rearrange("(p o) -> p o", o=1))

        xraw = {}

        def load_x(half, piece, start=0, width=HALF):
            if half not in xraw:
                xraw[half] = xraw_pool.tile([P, PASSES, PACK, HALF], BF16, name="xraw")
            g, u = divmod(piece, 2)
            first = (half % 2) * HALF
            nc.sync.dma_start(
                out=xraw[half][:, g, 2 * u : 2 * u + 2, start : start + width],
                in_=x_view[half // 2, :, g, u, :, first + start : first + start + width],
            )

        wv_raw = consts.tile([P, 1024], BF16)
        for g in range(PASSES):
            for block in range(BLOCKS):
                for u in range(2):
                    load_x(0, 2 * g + u, block * BLOCK, BLOCK)
            if g == 0:
                nc.sync.dma_start(out=wv_raw[:], in_=Wv)
        wk_raw = consts.tile([P, KEY_TILES, 1024], BF16)
        wk_view = Wk.rearrange("(p m) k -> p m k", m=KEY_TILES)
        for m in range(0, KEY_TILES, 2):
            nc.sync.dma_start(out=wk_raw[:, m : m + 2, :], in_=wk_view[:, m : m + 2, :])
        for piece in range(4):
            load_x(1, piece)

        scale_t = consts.tile([P, TILES], F32)
        bias_t = consts.tile([P, TILES], F32)
        std = consts.tile([P, KEY_TILES], F32)
        keys = slice(0, KEY_TILES)
        nc.vector.tensor_scalar_add(out=std[:], in0=prm[:, 4, keys], scalar1=EPS)
        nc.scalar.sqrt(out=std[:], in_=std[:])
        nc.vector.reciprocal(out=std[:], in_=std[:])
        nc.vector.tensor_mul(out=scale_t[:, keys], in0=std[:], in1=prm[:, 1, keys])
        nc.vector.tensor_sub(out=bias_t[:, keys], in0=prm[:, 0, keys], in1=prm[:, 3, keys])
        nc.vector.tensor_mul(out=bias_t[:, keys], in0=bias_t[:, keys], in1=scale_t[:, keys])
        nc.vector.tensor_add(out=bias_t[:, keys], in0=bias_t[:, keys], in1=prm[:, 2, keys])
        nc.vector.memset(scale_t[:, VALUE_TILE : VALUE_TILE + 1], 1.0)
        nc.vector.tensor_copy(out=bias_t[:, VALUE_TILE : VALUE_TILE + 1], in_=prm[:, 5, 0:1])

        grouped = {}
        x_codes = {}
        x_scales = {}

        def regroup_x(half, g, block, copy):
            if block == 0:
                grouped[half, g] = grouped_pool.tile(
                    [P, HALF, PACK], BF16, name="grouped", align_bytes=64
                )
            cols = slice(block * BLOCK, (block + 1) * BLOCK)
            copy(
                out=grouped[half, g][:, cols, :].rearrange("p (c i) t -> p c t i", i=4),
                in_=xraw[half][:, g, :, cols].rearrange("p t (c i) -> p c t i", i=4),
            )

        def quantise_x(half, g):
            if g == 0:
                x_codes[half] = xq_pool.tile([P, PASSES, HALF], U32, name="x_codes", align_bytes=64)
                x_scales[half] = xq_pool.tile([P, PASSES, HALF], U8, name="x_scales", align_bytes=64)
            flat = grouped[half, g][:].rearrange("p n t -> p (n t)")
            for first in range(0, HALF * PACK, QUANT_MAX):
                width = min(QUANT_MAX, HALF * PACK - first)
                words = slice(first // PACK, (first + width) // PACK)
                nc.vector.quantize_mx(
                    out=x_codes[half][:, g, words].bitcast(FP8X4),
                    scales=x_scales[half][:, g, words],
                    in_=flat[:, first : first + width],
                )

        w_codes = consts.tile([P, TILES, PASSES * P], U32, align_bytes=64)
        w_scales = consts.tile([P, TILES, PASSES * P], U8, align_bytes=64)

        def prepare_weights(m):
            rows = wv_raw[:] if m == VALUE_TILE else wk_raw[:, m, :]
            words = rows.bitcast(F32)
            turned = psum.tile([P, BANK], F32, tag="acc")
            for gu in range(PASSES * 2):
                nc.tensor.transpose(
                    turned[:, gu * P : (gu + 1) * P], words[:, gu * P : (gu + 1) * P], ident[:]
                )
            w_grouped = wstage.tile([P, PASSES, P, PACK], BF16, align_bytes=64)
            nc.scalar.copy(
                out=w_grouped[:].bitcast(F32),
                in_=turned[:].rearrange("q (g u c) -> q g c u", g=PASSES, u=2),
            )
            nc.vector.quantize_mx(
                out=w_codes[:, m, :].bitcast(FP8X4),
                scales=w_scales[:, m, :],
                in_=w_grouped[:].rearrange("q g c t -> q (g c t)"),
            )

        def project(half, tiles):
            kf = kf_pool.tile([P, len(tiles), HALF], F32, name="kf")
            for j, m in enumerate(tiles):
                for first in range(0, HALF, BANK):
                    width = min(BANK, HALF - first)
                    acc = psum.tile([P, BANK], F32, tag="acc")
                    for g in range(PASSES):
                        nc.tensor.matmul_mx(
                            out=acc[:, 0:width],
                            lhsT=w_codes[:, m, g * P : (g + 1) * P].bitcast(FP8X4),
                            lhsT_scale=w_scales[:, m, g * P : (g + 1) * P],
                            rhs=x_codes[half][:, g, first : first + width].bitcast(FP8X4),
                            rhs_scale=x_scales[half][:, g, first : first + width],
                            start=(g == 0),
                            stop=(g == PASSES - 1),
                        )
                    nc.scalar.activation(
                        out=kf[:, j, first : first + width],
                        in_=acc[:, 0:width],
                        func=ACT.Identity if m == VALUE_TILE else ACT.Relu,
                        bias=bias_t[:, m : m + 1],
                        scale=scale_t[:, m : m + 1],
                    )
            if tiles[0] != VALUE_TILE:
                first = (half % 2) * HALF
                nc.sync.dma_start(
                    out=kf_view[half // 2, :, tiles[0] : tiles[0] + len(tiles), first : first + HALF],
                    in_=kf[:],
                )
            return kf

        sums8 = {}
        sums6 = {}

        def add_row_pairs(work):
            kf = work["kf"]
            pairs = pool_tmp.tile([P, len(work["tiles"]) * HALF_ROWS // 2, SIDE], F32, name="row_pairs")
            rows = kf[:].rearrange("p n (a two w) -> p (n a) two w", two=2, w=SIDE)
            nc.vector.tensor_tensor(out=pairs[:], in0=rows[:, :, 0, :], in1=rows[:, :, 1, :], op=ADD)
            work["row_pairs"] = pairs

        def add_column_pairs(work):
            pairs = work["row_pairs"]
            quads = pool_tmp.tile([P, len(work["tiles"]) * HALF // 4], F32, name="quads")
            cols = pairs[:].rearrange("p a (c two) -> p (a c) two", two=2)
            nc.gpsimd.tensor_tensor(out=quads[:], in0=cols[:, :, 0], in1=cols[:, :, 1], op=ADD)
            work["quads"] = quads

        def sum_cells(work):
            half, tiles, quads = work["half"], work["tiles"], work["quads"]
            b, part = divmod(half, 2)
            if part == 0 and tiles[0] == VALUE_TILE:
                sums8[b] = sums_pool.tile([P, 2, TILES, 32], F32, name="sums8")
                sums6[b] = sums_pool.tile([P, 2, TILES, 18], F32, name="sums6")
            span = slice(tiles[0], tiles[0] + len(tiles))
            nc.vector.tensor_reduce(
                out=sums8[b][:, part, span, :].rearrange("p n (r c) -> p (n r) c", c=8),
                in_=quads[:].rearrange("p (r hi c wi) -> p r c hi wi", hi=3, c=8, wi=3),
                axis=AXIS.XY,
                op=ADD,
            )
            nc.vector.tensor_reduce(
                out=sums6[b][:, part, span, :].rearrange("p n (r c) -> p (n r) c", c=6),
                in_=quads[:].rearrange("p (r hi c wi) -> p r c hi wi", hi=4, c=6, wi=4),
                axis=AXIS.XY,
                op=ADD,
            )

        def finish_image(b):
            tok = sums_pool.tile([P, KEY_TILES * TOKENS + P], F32, name="tok")
            nc.vector.memset(tok[:, KEY_TILES * TOKENS :], 0.0)
            by_tile = tok[:, 0 : TILES * TOKENS].rearrange("p (m t) -> p m t", t=TOKENS)
            level8 = by_tile[:, :, AT8:TOKENS]
            level6 = by_tile[:, :, AT6:AT8]
            nc.scalar.mul(
                out=level6.rearrange("p m (h j) -> p h m j", h=2), in_=sums6[b][:], mul=1.0 / 64.0
            )
            nc.scalar.mul(
                out=level8.rearrange("p m (h j) -> p h m j", h=2), in_=sums8[b][:], mul=1.0 / 36.0
            )
            wide = sums_pool.tile([P, TILES, 18], F32, name="wide")
            nc.vector.tensor_reduce(
                out=wide[:], in_=level6.rearrange("p m (a wi) -> p m a wi", wi=2), axis=AXIS.X, op=ADD
            )
            cells3 = sums_pool.tile([P, TILES * 3, 3], F32, name="cells3")
            nc.vector.tensor_reduce(
                out=cells3[:],
                in_=wide[:].rearrange("p m (r hi c) -> p (m r) c hi", hi=2, c=3),
                axis=AXIS.X,
                op=ADD,
            )
            nine = cells3[:].rearrange("p (m r) c -> p m (r c)", m=TILES)
            nc.scalar.mul(out=by_tile[:, :, AT3:AT6], in_=nine, mul=0.25)
            whole = sums_pool.tile([P, TILES], F32, name="whole")
            nc.vector.tensor_reduce(out=whole[:], in_=nine, axis=AXIS.X, op=ADD)
            nc.scalar.mul(out=by_tile[:, :, 0:AT3], in_=whole[:].unsqueeze(2), mul=1.0 / 36.0)
            nc.sync.dma_start(out=keyp_view[b], in_=tok[:, 0 : KEY_TILES * TOKENS])
            return tok

        def store_value(b, tok):
            turned = psum.tile([P, P], F32, tag="value", bufs=1)
            nc.tensor.transpose(turned[:], tok[:, KEY_TILES * TOKENS :], ident[:])
            value = sums_pool.tile([P, P], F32, name="value")
            nc.scalar.copy(out=value[:], in_=turned[:])
            nc.sync.dma_start(out=out_2[b], in_=value[0:TOKENS, :])

        groups = [[VALUE_TILE]] + [[m, m + 1] for m in range(0, KEY_TILES, 2)]
        tile_order = [m for tiles in groups for m in tiles]

        for g in range(PASSES):
            regroup_x(0, g, 0, nc.vector.tensor_copy)
            regroup_x(0, g, 1, nc.vector.tensor_copy)
            regroup_x(0, g, 2, nc.scalar.copy)
            if g > 0:
                quantise_x(0, g - 1)
        prepare_weights(tile_order[0])
        quantise_x(0, PASSES - 1)

        previous = None
        before = None
        value_due = None
        for half in range(HALVES):
            following = half + 1
            for step, tiles in enumerate(groups):
                if half == 0 and step + 1 < len(groups):
                    for m in groups[step + 1]:
                        prepare_weights(m)
                if half + 2 < HALVES and step < 4:
                    load_x(half + 2, step)
                if following < HALVES and step >= 2 and step % 2 == 0:
                    quantise_x(following, step // 2 - 1)

                work = {"half": half, "tiles": tiles, "kf": project(half, tiles)}
                if value_due is not None:
                    store_value(value_due[0], value_due[1])
                    value_due = None

                if previous is not None:
                    add_column_pairs(previous)
                add_row_pairs(work)
                if before is not None:
                    sum_cells(before)
                    if before["half"] % 2 == 1 and before["tiles"] == groups[-1]:
                        b = before["half"] // 2
                        value_due = (b, finish_image(b))
                before = previous
                previous = work

                if following < HALVES and step < 2 * PASSES:
                    g = step // 2
                    regroup_x(following, g, step % 2, nc.scalar.copy if step % 2 == 0 else nc.vector.tensor_copy)
                    if step % 2 == 1:
                        regroup_x(following, g, 2, nc.vector.tensor_copy)

        add_column_pairs(previous)
        sum_cells(before)
        sum_cells(previous)
        store_value(IMAGES - 1, finish_image(IMAGES - 1))
